import numpy as np
import ml_dtypes

BF16 = ml_dtypes.bfloat16


def bf(x):
    return np.asarray(x, np.float32).astype(BF16)


def f32(x):
    return np.asarray(x, np.float32)


def f64(x):
    return np.asarray(x).astype(np.float64)


def striped(idx):
    return np.tile(idx.reshape(-1, 16).T, (8, 1))


D0, D1, T, S, N = 128, 128, 3, 2048, 1024


def sigmoid(v):
    return 1.0 / (1.0 + np.exp(-v))


def setup_inputs():
    return {
        "base": f32(np.random.standard_normal((T * D1, S))),
        "f1": f32(np.random.standard_normal((T * D1, N))),
        "nb": f32(np.random.standard_normal((T * D1, N))),
        "nodes": bf(np.random.standard_normal((D0, N))),
        "w_gate": bf(np.random.standard_normal((D0, D1)) / np.sqrt(D0)),
        "b_gate": f32(0.5 * np.random.standard_normal((D1, 1))),
        "hs": f32(0.5 + 0.1 * np.random.standard_normal((D1, 1))),
        "hb": f32(0.5 + 0.1 * np.random.standard_normal((D1, 1))),
        "wv": f32(0.5 * np.random.standard_normal((D1, 1))),
        "offs": striped(np.random.permutation(S)[:N]),
    }


def reference(base, f1, nb, nodes, w_gate, b_gate, hs, hb, wv, offs):
    idx = offs[:16].T.reshape(-1)
    a = f64(f1).reshape(T, D1, N)
    rel = a - f64(nb).reshape(T, D1, N)
    nrm = np.sqrt((rel * rel).sum(axis=0))
    upd = rel / nrm * (nrm * f64(hs) + f64(hb)) * f64(wv)
    gate = sigmoid(f64(w_gate).T @ f64(nodes) + f64(b_gate))
    out = f64(base).copy()
    out[:, idx] = ((a + upd) * gate).reshape(T * D1, N)
    return out

@@ -1,0 +1,101 @@
+import concourse.mybir as mybir
+
+F32 = mybir.dt.float32
+BF16 = mybir.dt.bfloat16
+U16 = mybir.dt.uint16
+ALU = mybir.AluOpType
+ACT = mybir.ActivationFunctionType
+
+P = 128
+T = 3
+S = 2048
+N = 1024
+C = 512
+CHUNKS = N // C
+FLOPS = 2 * P * P * N
+
+
+def tile_egnn_kernel(tc, base, f1, nb, nodes, w_gate, b_gate, hs, hb, wv, offs, out):
+    nc = tc.nc
+    f1_dtn = f1.rearrange("(t d) n -> d t n", t=T)
+    nb_dtn = nb.rearrange("(t d) n -> d t n", t=T)
+
+    with (
+        tc.tile_pool(name="held", bufs=1) as held,
+        tc.tile_pool(name="work", bufs=2) as work,
+        tc.psum_pool(name="psum", bufs=2) as psum,
+    ):
+        offsets = held.tile([P, N // 16], U16, name="offsets")
+        nc.sync.dma_start(offsets[:], offs)
+
+        w_sb = held.tile([P, P], BF16, name="w_sb")
+        nc.sync.dma_start(w_sb[:], w_gate)
+        nodes_sb = held.tile([P, N], BF16, name="nodes_sb")
+        nc.sync.dma_start(nodes_sb[:], nodes)
+        b_sb = held.tile([P, 1], F32, name="b_sb")
+        nc.sync.dma_start(b_sb[:], b_gate)
+        hs_sb = held.tile([P, 1], F32, name="hs_sb")
+        nc.sync.dma_start(hs_sb[:], hs)
+        hb_sb = held.tile([P, 1], F32, name="hb_sb")
+        nc.sync.dma_start(hb_sb[:], hb)
+        wv_sb = held.tile([P, 1], F32, name="wv_sb")
+        nc.sync.dma_start(wv_sb[:], wv)
+
+        f1_sb = []
+        nb_sb = []
+        windows = []
+        for c in range(CHUNKS):
+            cols = slice(c * C, (c + 1) * C)
+            f1_c = held.tile([P, T, C], F32, name=f"f1_{c}")
+            nc.sync.dma_start(f1_c[:], f1_dtn[:, :, cols])
+            nb_c = held.tile([P, T, C], F32, name=f"nb_{c}")
+            nc.sync.dma_start(nb_c[:], nb_dtn[:, :, cols])
+            f1_sb.append(f1_c)
+            nb_sb.append(nb_c)
+            if c == 0:
+                for t in range(T):
+                    window = held.tile([P, S], F32, name=f"window{t}")
+                    nc.sync.dma_start(window[:], base[t * P : (t + 1) * P, :])
+                    windows.append(window)
+
+        slope = held.tile([P, 1], F32, name="slope")
+        nc.vector.tensor_tensor(slope[:], hb_sb[:], wv_sb[:], ALU.mult)
+        level = held.tile([P, 1], F32, name="level")
+        nc.vector.tensor_tensor(level[:], hs_sb[:], wv_sb[:], ALU.mult)
+
+        for c in range(CHUNKS):
+            cols = slice(c * C, (c + 1) * C)
+
+            logits = psum.tile([P, C], F32, name="logits")
+            nc.tensor.matmul(logits[:], w_sb[:], nodes_sb[:, cols], start=True, stop=True)
+            gate = work.tile([P, C], F32, name="gate")
+            nc.scalar.activation(gate[:], logits[:], ACT.Sigmoid, bias=b_sb[:])
+
+            rel = work.tile([P, T, C], F32, name="rel")
+            nc.vector.tensor_tensor(rel[:], f1_sb[c][:], nb_sb[c][:], ALU.subtract)
+            squares = work.tile([P, T, C], F32, name="squares")
+            nc.scalar.activation(squares[:], rel[:], ACT.Square)
+            two = work.tile([P, C], F32, name="two")
+            nc.vector.tensor_tensor(two[:], squares[:, 0, :], squares[:, 1, :], ALU.add)
+            three = work.tile([P, C], F32, name="three")
+            nc.vector.tensor_tensor(three[:], two[:], squares[:, 2, :], ALU.add)
+            inv_nrm = work.tile([P, C], F32, name="inv_nrm")
+            nc.scalar.activation(inv_nrm[:], three[:], ACT.Abs_reciprocal_sqrt)
+            factor = work.tile([P, C], F32, name="factor")
+            nc.scalar.activation(factor[:], inv_nrm[:], ACT.Identity, bias=level[:], scale=slope[:])
+
+            upd = work.tile([P, T, C], F32, name="upd")
+            nc.vector.tensor_tensor(
+                upd[:], rel[:], factor[:].unsqueeze(1).to_broadcast([P, T, C]), ALU.mult
+            )
+            moved = work.tile([P, T, C], F32, name="moved")
+            nc.vector.tensor_tensor(moved[:], f1_sb[c][:], upd[:], ALU.add)
+
+            piece = offsets[:, c * (C // 16) : (c + 1) * (C // 16)]
+            for t in range(T):
+                nc.vector.tensor_tensor(
+                    windows[t][:].indirect(piece), moved[:, t, :], gate[:], ALU.mult
+                )
+
+        for t in range(T):
+            nc.sync.dma_start(out[t * P : (t + 1) * P, :], windows[t][:])

@@ -11,7 +11,9 @@ T = 3
 S = 2048
 N = 1024
 C = 512
-CHUNKS = N // C
+PIECES = N // C
+B = 256
+BLOCKS = N // B
 FLOPS = 2 * P * P * N
 
 
@@ -22,8 +24,8 @@ def tile_egnn_kernel(tc, base, f1, nb, nodes, w_gate, b_gate, hs, hb, wv, offs, 
 
     with (
         tc.tile_pool(name="held", bufs=1) as held,
-        tc.tile_pool(name="work", bufs=2) as work,
-        tc.psum_pool(name="psum", bufs=2) as psum,
+        tc.tile_pool(name="work", bufs=BLOCKS) as work,
+        tc.psum_pool(name="psum", bufs=PIECES) as psum,
     ):
         offsets = held.tile([P, N // 16], U16, name="offsets")
         nc.sync.dma_start(offsets[:], offs)
@@ -33,69 +35,68 @@ def tile_egnn_kernel(tc, base, f1, nb, nodes, w_gate, b_gate, hs, hb, wv, offs, 
         nodes_sb = held.tile([P, N], BF16, name="nodes_sb")
         nc.sync.dma_start(nodes_sb[:], nodes)
         b_sb = held.tile([P, 1], F32, name="b_sb")
-        nc.sync.dma_start(b_sb[:], b_gate)
+        nc.scalar.dma_start(b_sb[:], b_gate)
         hs_sb = held.tile([P, 1], F32, name="hs_sb")
-        nc.sync.dma_start(hs_sb[:], hs)
+        nc.scalar.dma_start(hs_sb[:], hs)
         hb_sb = held.tile([P, 1], F32, name="hb_sb")
-        nc.sync.dma_start(hb_sb[:], hb)
+        nc.scalar.dma_start(hb_sb[:], hb)
         wv_sb = held.tile([P, 1], F32, name="wv_sb")
-        nc.sync.dma_start(wv_sb[:], wv)
-
+        nc.scalar.dma_start(wv_sb[:], wv)
         f1_sb = []
         nb_sb = []
+        for b in range(BLOCKS):
+            cols = slice(b * B, (b + 1) * B)
+            f1_b = work.tile([P, T, B], F32, name="f1_b")
+            nc.sync.dma_start(f1_b[:], f1_dtn[:, :, cols])
+            nb_b = work.tile([P, T, B], F32, name="nb_b")
+            nc.sync.dma_start(nb_b[:], nb_dtn[:, :, cols])
+            f1_sb.append(f1_b)
+            nb_sb.append(nb_b)
         windows = []
-        for c in range(CHUNKS):
-            cols = slice(c * C, (c + 1) * C)
-            f1_c = held.tile([P, T, C], F32, name=f"f1_{c}")
-            nc.sync.dma_start(f1_c[:], f1_dtn[:, :, cols])
-            nb_c = held.tile([P, T, C], F32, name=f"nb_{c}")
-            nc.sync.dma_start(nb_c[:], nb_dtn[:, :, cols])
-            f1_sb.append(f1_c)
-            nb_sb.append(nb_c)
-            if c == 0:
-                for t in range(T):
-                    window = held.tile([P, S], F32, name=f"window{t}")
-                    nc.sync.dma_start(window[:], base[t * P : (t + 1) * P, :])
-                    windows.append(window)
+        for t in range(T):
+            window = held.tile([P, S], F32, name=f"window{t}")
+            nc.sync.dma_start(window[:], base[t * P : (t + 1) * P, :])
+            windows.append(window)
+
+        gates = []
+        for c in range(PIECES):
+            logits = psum.tile([P, C], F32, name="logits")
+            nc.tensor.matmul(logits[:], w_sb[:], nodes_sb[:, c * C : (c + 1) * C], start=True, stop=True)
+            gate = held.tile([P, C], F32, name=f"gate{c}")
+            nc.scalar.activation(gate[:], logits[:], ACT.Sigmoid, bias=b_sb[:])
+            gates.append(gate)
 
         slope = held.tile([P, 1], F32, name="slope")
         nc.vector.tensor_tensor(slope[:], hb_sb[:], wv_sb[:], ALU.mult)
         level = held.tile([P, 1], F32, name="level")
         nc.vector.tensor_tensor(level[:], hs_sb[:], wv_sb[:], ALU.mult)
 
-        for c in range(CHUNKS):
-            cols = slice(c * C, (c + 1) * C)
-
-            logits = psum.tile([P, C], F32, name="logits")
-            nc.tensor.matmul(logits[:], w_sb[:], nodes_sb[:, cols], start=True, stop=True)
-            gate = work.tile([P, C], F32, name="gate")
-            nc.scalar.activation(gate[:], logits[:], ACT.Sigmoid, bias=b_sb[:])
-
-            rel = work.tile([P, T, C], F32, name="rel")
-            nc.vector.tensor_tensor(rel[:], f1_sb[c][:], nb_sb[c][:], ALU.subtract)
-            squares = work.tile([P, T, C], F32, name="squares")
+        moved = [held.tile([P, T, C], F32, name=f"moved{c}") for c in range(PIECES)]
+        for b in range(BLOCKS):
+            rel = work.tile([P, T, B], F32, name="rel")
+            nc.vector.tensor_tensor(rel[:], f1_sb[b][:], nb_sb[b][:], ALU.subtract)
+            squares = work.tile([P, T, B], F32, name="squares")
             nc.scalar.activation(squares[:], rel[:], ACT.Square)
-            two = work.tile([P, C], F32, name="two")
+            two = work.tile([P, B], F32, name="two")
             nc.vector.tensor_tensor(two[:], squares[:, 0, :], squares[:, 1, :], ALU.add)
-            three = work.tile([P, C], F32, name="three")
+            three = work.tile([P, B], F32, name="three")
             nc.vector.tensor_tensor(three[:], two[:], squares[:, 2, :], ALU.add)
-            inv_nrm = work.tile([P, C], F32, name="inv_nrm")
+            inv_nrm = work.tile([P, B], F32, name="inv_nrm")
             nc.scalar.activation(inv_nrm[:], three[:], ACT.Abs_reciprocal_sqrt)
-            factor = work.tile([P, C], F32, name="factor")
+            factor = work.tile([P, B], F32, name="factor")
             nc.scalar.activation(factor[:], inv_nrm[:], ACT.Identity, bias=level[:], scale=slope[:])
-
-            upd = work.tile([P, T, C], F32, name="upd")
+            upd = work.tile([P, T, B], F32, name="upd")
             nc.vector.tensor_tensor(
-                upd[:], rel[:], factor[:].unsqueeze(1).to_broadcast([P, T, C]), ALU.mult
+                upd[:], rel[:], factor[:].unsqueeze(1).to_broadcast([P, T, B]), ALU.mult
             )
-            moved = work.tile([P, T, C], F32, name="moved")
-            nc.vector.tensor_tensor(moved[:], f1_sb[c][:], upd[:], ALU.add)
+            c, half = divmod(b * B, C)
+            nc.vector.tensor_tensor(moved[c][:, :, half : half + B], f1_sb[b][:], upd[:], ALU.add)
 
+        for c in range(PIECES):
             piece = offsets[:, c * (C // 16) : (c + 1) * (C // 16)]
             for t in range(T):
                 nc.vector.tensor_tensor(
-                    windows[t][:].indirect(piece), moved[:, t, :], gate[:], ALU.mult
+                    windows[t][:].indirect(piece), moved[c][:, t, :], gates[c][:], ALU.mult
                 )
-
-        for t in range(T):
-            nc.sync.dma_start(out[t * P : (t + 1) * P, :], windows[t][:])
+                if c == PIECES - 1:
+                    nc.sync.dma_start(out[t * P : (t + 1) * P, :], windows[t][:])

@@ -1,4 +1,5 @@
 import concourse.mybir as mybir
+from concourse.masks import make_identity
 
 F32 = mybir.dt.float32
 BF16 = mybir.dt.bfloat16
@@ -25,7 +26,8 @@ def tile_egnn_kernel(tc, base, f1, nb, nodes, w_gate, b_gate, hs, hb, wv, offs, 
     with (
         tc.tile_pool(name="held", bufs=1) as held,
         tc.tile_pool(name="work", bufs=BLOCKS) as work,
-        tc.psum_pool(name="psum", bufs=PIECES) as psum,
+        tc.psum_pool(name="psum", bufs=2) as psum,
+        tc.psum_pool(name="psum_sums", bufs=6) as psum_sums,
     ):
         offsets = held.tile([P, N // 16], U16, name="offsets")
         nc.sync.dma_start(offsets[:], offs)
@@ -60,7 +62,7 @@ def tile_egnn_kernel(tc, base, f1, nb, nodes, w_gate, b_gate, hs, hb, wv, offs, 
 
         gates = []
         for c in range(PIECES):
-            logits = psum.tile([P, C], F32, name="logits")
+            logits = psum.tile([P, C], F32, name="logits", tag="bank")
             nc.tensor.matmul(logits[:], w_sb[:], nodes_sb[:, c * C : (c + 1) * C], start=True, stop=True)
             gate = held.tile([P, C], F32, name=f"gate{c}")
             nc.scalar.activation(gate[:], logits[:], ACT.Sigmoid, bias=b_sb[:])
@@ -71,18 +73,20 @@ def tile_egnn_kernel(tc, base, f1, nb, nodes, w_gate, b_gate, hs, hb, wv, offs, 
         level = held.tile([P, 1], F32, name="level")
         nc.vector.tensor_tensor(level[:], hs_sb[:], wv_sb[:], ALU.mult)
 
+        ident = held.tile([P, P], F32, name="ident")
+        make_identity(nc, ident[:])
+
         moved = [held.tile([P, T, C], F32, name=f"moved{c}") for c in range(PIECES)]
         for b in range(BLOCKS):
             rel = work.tile([P, T, B], F32, name="rel")
             nc.vector.tensor_tensor(rel[:], f1_sb[b][:], nb_sb[b][:], ALU.subtract)
             squares = work.tile([P, T, B], F32, name="squares")
             nc.scalar.activation(squares[:], rel[:], ACT.Square)
-            two = work.tile([P, B], F32, name="two")
-            nc.vector.tensor_tensor(two[:], squares[:, 0, :], squares[:, 1, :], ALU.add)
-            three = work.tile([P, B], F32, name="three")
-            nc.vector.tensor_tensor(three[:], two[:], squares[:, 2, :], ALU.add)
+            sumsq = psum.tile([P, B], F32, name="sumsq", tag="bank")
+            for t in range(T):
+                nc.tensor.matmul(sumsq[:], ident[:], squares[:, t, :], start=(t == 0), stop=(t == T - 1))
             inv_nrm = work.tile([P, B], F32, name="inv_nrm")
-            nc.scalar.activation(inv_nrm[:], three[:], ACT.Abs_reciprocal_sqrt)
+            nc.scalar.activation(inv_nrm[:], sumsq[:], ACT.Abs_reciprocal_sqrt)
             factor = work.tile([P, B], F32, name="factor")
             nc.scalar.activation(factor[:], inv_nrm[:], ACT.Identity, bias=level[:], scale=slope[:])
             upd = work.tile([P, T, B], F32, name="upd")
@@ -90,7 +94,11 @@ def tile_egnn_kernel(tc, base, f1, nb, nodes, w_gate, b_gate, hs, hb, wv, offs, 
                 upd[:], rel[:], factor[:].unsqueeze(1).to_broadcast([P, T, B]), ALU.mult
             )
             c, half = divmod(b * B, C)
-            nc.vector.tensor_tensor(moved[c][:, :, half : half + B], f1_sb[b][:], upd[:], ALU.add)
+            for t in range(T):
+                total = psum_sums.tile([P, B], F32, name="total")
+                nc.tensor.matmul(total[:], ident[:], f1_sb[b][:, t, :], start=True, stop=False)
+                nc.tensor.matmul(total[:], ident[:], upd[:, t, :], start=False, stop=True)
+                nc.scalar.copy(moved[c][:, t, half : half + B], total[:])
 
         for c in range(PIECES):
             piece = offsets[:, c * (C // 16) : (c + 1) * (C // 16)]

@@ -1,5 +1,4 @@
 import concourse.mybir as mybir
-from concourse.masks import make_identity
 
 F32 = mybir.dt.float32
 BF16 = mybir.dt.bfloat16
@@ -26,8 +25,7 @@ def tile_egnn_kernel(tc, base, f1, nb, nodes, w_gate, b_gate, hs, hb, wv, offs, 
     with (
         tc.tile_pool(name="held", bufs=1) as held,
         tc.tile_pool(name="work", bufs=BLOCKS) as work,
-        tc.psum_pool(name="psum", bufs=2) as psum,
-        tc.psum_pool(name="psum_sums", bufs=6) as psum_sums,
+        tc.psum_pool(name="psum", bufs=PIECES) as psum,
     ):
         offsets = held.tile([P, N // 16], U16, name="offsets")
         nc.sync.dma_start(offsets[:], offs)
@@ -62,7 +60,7 @@ def tile_egnn_kernel(tc, base, f1, nb, nodes, w_gate, b_gate, hs, hb, wv, offs, 
 
         gates = []
         for c in range(PIECES):
-            logits = psum.tile([P, C], F32, name="logits", tag="bank")
+            logits = psum.tile([P, C], F32, name="logits")
             nc.tensor.matmul(logits[:], w_sb[:], nodes_sb[:, c * C : (c + 1) * C], start=True, stop=True)
             gate = held.tile([P, C], F32, name=f"gate{c}")
             nc.scalar.activation(gate[:], logits[:], ACT.Sigmoid, bias=b_sb[:])
@@ -73,20 +71,18 @@ def tile_egnn_kernel(tc, base, f1, nb, nodes, w_gate, b_gate, hs, hb, wv, offs, 
         level = held.tile([P, 1], F32, name="level")
         nc.vector.tensor_tensor(level[:], hs_sb[:], wv_sb[:], ALU.mult)
 
-        ident = held.tile([P, P], F32, name="ident")
-        make_identity(nc, ident[:])
-
         moved = [held.tile([P, T, C], F32, name=f"moved{c}") for c in range(PIECES)]
         for b in range(BLOCKS):
             rel = work.tile([P, T, B], F32, name="rel")
             nc.vector.tensor_tensor(rel[:], f1_sb[b][:], nb_sb[b][:], ALU.subtract)
             squares = work.tile([P, T, B], F32, name="squares")
             nc.scalar.activation(squares[:], rel[:], ACT.Square)
-            sumsq = psum.tile([P, B], F32, name="sumsq", tag="bank")
-            for t in range(T):
-                nc.tensor.matmul(sumsq[:], ident[:], squares[:, t, :], start=(t == 0), stop=(t == T - 1))
+            two = work.tile([P, B], F32, name="two")
+            nc.vector.tensor_tensor(two[:], squares[:, 0, :], squares[:, 1, :], ALU.add)
+            three = work.tile([P, B], F32, name="three")
+            nc.vector.tensor_tensor(three[:], two[:], squares[:, 2, :], ALU.add)
             inv_nrm = work.tile([P, B], F32, name="inv_nrm")
-            nc.scalar.activation(inv_nrm[:], sumsq[:], ACT.Abs_reciprocal_sqrt)
+            nc.scalar.activation(inv_nrm[:], three[:], ACT.Abs_reciprocal_sqrt)
             factor = work.tile([P, B], F32, name="factor")
             nc.scalar.activation(factor[:], inv_nrm[:], ACT.Identity, bias=level[:], scale=slope[:])
             upd = work.tile([P, T, B], F32, name="upd")
@@ -94,11 +90,7 @@ def tile_egnn_kernel(tc, base, f1, nb, nodes, w_gate, b_gate, hs, hb, wv, offs, 
                 upd[:], rel[:], factor[:].unsqueeze(1).to_broadcast([P, T, B]), ALU.mult
             )
             c, half = divmod(b * B, C)
-            for t in range(T):
-                total = psum_sums.tile([P, B], F32, name="total")
-                nc.tensor.matmul(total[:], ident[:], f1_sb[b][:, t, :], start=True, stop=False)
-                nc.tensor.matmul(total[:], ident[:], upd[:, t, :], start=False, stop=True)
-                nc.scalar.copy(moved[c][:, t, half : half + B], total[:])
+            nc.gpsimd.tensor_tensor(moved[c][:, :, half : half + B], f1_sb[b][:], upd[:], ALU.add)
 
         for c in range(PIECES):
             piece = offsets[:, c * (C // 16) : (c + 1) * (C // 16)]

@@ -1,4 +1,5 @@
 import concourse.mybir as mybir
+from concourse.masks import make_identity
 
 F32 = mybir.dt.float32
 BF16 = mybir.dt.bfloat16
@@ -25,7 +26,8 @@ def tile_egnn_kernel(tc, base, f1, nb, nodes, w_gate, b_gate, hs, hb, wv, offs, 
     with (
         tc.tile_pool(name="held", bufs=1) as held,
         tc.tile_pool(name="work", bufs=BLOCKS) as work,
-        tc.psum_pool(name="psum", bufs=PIECES) as psum,
+        tc.psum_pool(name="psum", bufs=2) as psum,
+        tc.psum_pool(name="psum_sums", bufs=6) as psum_sums,
     ):
         offsets = held.tile([P, N // 16], U16, name="offsets")
         nc.sync.dma_start(offsets[:], offs)
@@ -60,7 +62,7 @@ def tile_egnn_kernel(tc, base, f1, nb, nodes, w_gate, b_gate, hs, hb, wv, offs, 
 
         gates = []
         for c in range(PIECES):
-            logits = psum.tile([P, C], F32, name="logits")
+            logits = psum.tile([P, C], F32, name="logits", tag="bank")
             nc.tensor.matmul(logits[:], w_sb[:], nodes_sb[:, c * C : (c + 1) * C], start=True, stop=True)
             gate = held.tile([P, C], F32, name=f"gate{c}")
             nc.scalar.activation(gate[:], logits[:], ACT.Sigmoid, bias=b_sb[:])
@@ -71,26 +73,41 @@ def tile_egnn_kernel(tc, base, f1, nb, nodes, w_gate, b_gate, hs, hb, wv, offs, 
         level = held.tile([P, 1], F32, name="level")
         nc.vector.tensor_tensor(level[:], hs_sb[:], wv_sb[:], ALU.mult)
 
+        ident = held.tile([P, P], F32, name="ident")
+        make_identity(nc, ident[:])
+
         moved = [held.tile([P, T, C], F32, name=f"moved{c}") for c in range(PIECES)]
         for b in range(BLOCKS):
             rel = work.tile([P, T, B], F32, name="rel")
             nc.vector.tensor_tensor(rel[:], f1_sb[b][:], nb_sb[b][:], ALU.subtract)
             squares = work.tile([P, T, B], F32, name="squares")
             nc.scalar.activation(squares[:], rel[:], ACT.Square)
-            two = work.tile([P, B], F32, name="two")
-            nc.vector.tensor_tensor(two[:], squares[:, 0, :], squares[:, 1, :], ALU.add)
-            three = work.tile([P, B], F32, name="three")
-            nc.vector.tensor_tensor(three[:], two[:], squares[:, 2, :], ALU.add)
+            c, half = divmod(b * B, C)
+            if c == 0:
+                two = work.tile([P, B], F32, name="two")
+                nc.vector.tensor_tensor(two[:], squares[:, 0, :], squares[:, 1, :], ALU.add)
+                sumsq = work.tile([P, B], F32, name="three")
+                nc.vector.tensor_tensor(sumsq[:], two[:], squares[:, 2, :], ALU.add)
+            else:
+                sumsq = psum.tile([P, B], F32, name="sumsq", tag="bank")
+                for t in range(T):
+                    nc.tensor.matmul(sumsq[:], ident[:], squares[:, t, :], start=(t == 0), stop=(t == T - 1))
             inv_nrm = work.tile([P, B], F32, name="inv_nrm")
-            nc.scalar.activation(inv_nrm[:], three[:], ACT.Abs_reciprocal_sqrt)
+            nc.scalar.activation(inv_nrm[:], sumsq[:], ACT.Abs_reciprocal_sqrt)
             factor = work.tile([P, B], F32, name="factor")
             nc.scalar.activation(factor[:], inv_nrm[:], ACT.Identity, bias=level[:], scale=slope[:])
             upd = work.tile([P, T, B], F32, name="upd")
             nc.vector.tensor_tensor(
                 upd[:], rel[:], factor[:].unsqueeze(1).to_broadcast([P, T, B]), ALU.mult
             )
-            c, half = divmod(b * B, C)
-            nc.gpsimd.tensor_tensor(moved[c][:, :, half : half + B], f1_sb[b][:], upd[:], ALU.add)
+            if c == 0:
+                nc.vector.tensor_tensor(moved[c][:, :, half : half + B], f1_sb[b][:], upd[:], ALU.add)
+            else:
+                for t in range(T):
+                    total = psum_sums.tile([P, B], F32, name="total")
+                    nc.tensor.matmul(total[:], ident[:], f1_sb[b][:, t, :], start=True, stop=False)
+                    nc.tensor.matmul(total[:], ident[:], upd[:, t, :], start=False, stop=True)
+                    nc.scalar.copy(moved[c][:, t, half : half + B], total[:])
 
         for c in range(PIECES):
             piece = offsets[:, c * (C // 16) : (c + 1) * (C // 16)]

@@ -11,10 +11,11 @@ P = 128
 T = 3
 S = 2048
 N = 1024
-C = 512
-PIECES = N // C
-B = 256
-BLOCKS = N // B
+PIECE = 512
+PIECES = N // PIECE
+BLOCK = 256
+BLOCKS = N // BLOCK
+BLOCKS_IN_PIECE = PIECE // BLOCK
 FLOPS = 2 * P * P * N
 
 
@@ -27,7 +28,7 @@ def tile_egnn_kernel(tc, base, f1, nb, nodes, w_gate, b_gate, hs, hb, wv, offs, 
         tc.tile_pool(name="held", bufs=1) as held,
         tc.tile_pool(name="work", bufs=BLOCKS) as work,
         tc.psum_pool(name="psum", bufs=2) as psum,
-        tc.psum_pool(name="psum_sums", bufs=6) as psum_sums,
+        tc.psum_pool(name="psum_moved", bufs=BLOCKS_IN_PIECE * T) as psum_moved,
     ):
         offsets = held.tile([P, N // 16], U16, name="offsets")
         nc.sync.dma_start(offsets[:], offs)
@@ -46,14 +47,14 @@ def tile_egnn_kernel(tc, base, f1, nb, nodes, w_gate, b_gate, hs, hb, wv, offs, 
         nc.scalar.dma_start(wv_sb[:], wv)
         f1_sb = []
         nb_sb = []
-        for b in range(BLOCKS):
-            cols = slice(b * B, (b + 1) * B)
-            f1_b = work.tile([P, T, B], F32, name="f1_b")
-            nc.sync.dma_start(f1_b[:], f1_dtn[:, :, cols])
-            nb_b = work.tile([P, T, B], F32, name="nb_b")
-            nc.sync.dma_start(nb_b[:], nb_dtn[:, :, cols])
-            f1_sb.append(f1_b)
-            nb_sb.append(nb_b)
+        for block in range(BLOCKS):
+            cols = slice(block * BLOCK, (block + 1) * BLOCK)
+            f1_block = work.tile([P, T, BLOCK], F32, name="f1_block")
+            nc.sync.dma_start(f1_block[:], f1_dtn[:, :, cols])
+            nb_block = work.tile([P, T, BLOCK], F32, name="nb_block")
+            nc.sync.dma_start(nb_block[:], nb_dtn[:, :, cols])
+            f1_sb.append(f1_block)
+            nb_sb.append(nb_block)
         windows = []
         for t in range(T):
             window = held.tile([P, S], F32, name=f"window{t}")
@@ -61,10 +62,11 @@ def tile_egnn_kernel(tc, base, f1, nb, nodes, w_gate, b_gate, hs, hb, wv, offs, 
             windows.append(window)
 
         gates = []
-        for c in range(PIECES):
-            logits = psum.tile([P, C], F32, name="logits", tag="bank")
-            nc.tensor.matmul(logits[:], w_sb[:], nodes_sb[:, c * C : (c + 1) * C], start=True, stop=True)
-            gate = held.tile([P, C], F32, name=f"gate{c}")
+        for piece in range(PIECES):
+            cols = slice(piece * PIECE, (piece + 1) * PIECE)
+            logits = psum.tile([P, PIECE], F32, name="logits", tag="bank")
+            nc.tensor.matmul(logits[:], w_sb[:], nodes_sb[:, cols], start=True, stop=True)
+            gate = held.tile([P, PIECE], F32, name=f"gate{piece}")
             nc.scalar.activation(gate[:], logits[:], ACT.Sigmoid, bias=b_sb[:])
             gates.append(gate)
 
@@ -76,44 +78,45 @@ def tile_egnn_kernel(tc, base, f1, nb, nodes, w_gate, b_gate, hs, hb, wv, offs, 
         ident = held.tile([P, P], F32, name="ident")
         make_identity(nc, ident[:])
 
-        moved = [held.tile([P, T, C], F32, name=f"moved{c}") for c in range(PIECES)]
-        for b in range(BLOCKS):
-            rel = work.tile([P, T, B], F32, name="rel")
-            nc.vector.tensor_tensor(rel[:], f1_sb[b][:], nb_sb[b][:], ALU.subtract)
-            squares = work.tile([P, T, B], F32, name="squares")
+        moved = [held.tile([P, T, PIECE], F32, name=f"moved{piece}") for piece in range(PIECES)]
+        for block in range(BLOCKS):
+            piece, first = divmod(block * BLOCK, PIECE)
+            f1_block = f1_sb[block]
+            rel = work.tile([P, T, BLOCK], F32, name="rel")
+            nc.vector.tensor_tensor(rel[:], f1_block[:], nb_sb[block][:], ALU.subtract)
+            squares = work.tile([P, T, BLOCK], F32, name="squares")
             nc.scalar.activation(squares[:], rel[:], ACT.Square)
-            c, half = divmod(b * B, C)
-            if c == 0:
-                two = work.tile([P, B], F32, name="two")
-                nc.vector.tensor_tensor(two[:], squares[:, 0, :], squares[:, 1, :], ALU.add)
-                sumsq = work.tile([P, B], F32, name="three")
-                nc.vector.tensor_tensor(sumsq[:], two[:], squares[:, 2, :], ALU.add)
+            if piece == 0:
+                pair = work.tile([P, BLOCK], F32, name="pair")
+                nc.vector.tensor_tensor(pair[:], squares[:, 0, :], squares[:, 1, :], ALU.add)
+                sumsq = work.tile([P, BLOCK], F32, name="sumsq_sb")
+                nc.vector.tensor_tensor(sumsq[:], pair[:], squares[:, 2, :], ALU.add)
             else:
-                sumsq = psum.tile([P, B], F32, name="sumsq", tag="bank")
+                sumsq = psum.tile([P, BLOCK], F32, name="sumsq_ps", tag="bank")
                 for t in range(T):
                     nc.tensor.matmul(sumsq[:], ident[:], squares[:, t, :], start=(t == 0), stop=(t == T - 1))
-            inv_nrm = work.tile([P, B], F32, name="inv_nrm")
+            inv_nrm = work.tile([P, BLOCK], F32, name="inv_nrm")
             nc.scalar.activation(inv_nrm[:], sumsq[:], ACT.Abs_reciprocal_sqrt)
-            factor = work.tile([P, B], F32, name="factor")
+            factor = work.tile([P, BLOCK], F32, name="factor")
             nc.scalar.activation(factor[:], inv_nrm[:], ACT.Identity, bias=level[:], scale=slope[:])
-            upd = work.tile([P, T, B], F32, name="upd")
+            upd = work.tile([P, T, BLOCK], F32, name="upd")
             nc.vector.tensor_tensor(
-                upd[:], rel[:], factor[:].unsqueeze(1).to_broadcast([P, T, B]), ALU.mult
+                upd[:], rel[:], factor[:].unsqueeze(1).to_broadcast([P, T, BLOCK]), ALU.mult
             )
-            if c == 0:
-                nc.vector.tensor_tensor(moved[c][:, :, half : half + B], f1_sb[b][:], upd[:], ALU.add)
+            if piece == 0:
+                nc.vector.tensor_tensor(moved[piece][:, :, first : first + BLOCK], f1_block[:], upd[:], ALU.add)
             else:
                 for t in range(T):
-                    total = psum_sums.tile([P, B], F32, name="total")
-                    nc.tensor.matmul(total[:], ident[:], f1_sb[b][:, t, :], start=True, stop=False)
-                    nc.tensor.matmul(total[:], ident[:], upd[:, t, :], start=False, stop=True)
-                    nc.scalar.copy(moved[c][:, t, half : half + B], total[:])
+                    moved_ps = psum_moved.tile([P, BLOCK], F32, name="moved_ps")
+                    nc.tensor.matmul(moved_ps[:], ident[:], f1_block[:, t, :], start=True, stop=False)
+                    nc.tensor.matmul(moved_ps[:], ident[:], upd[:, t, :], start=False, stop=True)
+                    nc.scalar.copy(moved[piece][:, t, first : first + BLOCK], moved_ps[:])
 
-        for c in range(PIECES):
-            piece = offsets[:, c * (C // 16) : (c + 1) * (C // 16)]
+        for piece in range(PIECES):
+            piece_offsets = offsets[:, piece * (PIECE // 16) : (piece + 1) * (PIECE // 16)]
             for t in range(T):
                 nc.vector.tensor_tensor(
-                    windows[t][:].indirect(piece), moved[c][:, t, :], gates[c][:], ALU.mult
+                    windows[t][:].indirect(piece_offsets), moved[piece][:, t, :], gates[piece][:], ALU.mult
                 )
-                if c == PIECES - 1:
+                if piece == PIECES - 1:
                     nc.sync.dma_start(out[t * P : (t + 1) * P, :], windows[t][:])

@@ -11,11 +11,12 @@ P = 128
 T = 3
 S = 2048
 N = 1024
-PIECE = 512
-PIECES = N // PIECE
 BLOCK = 256
 BLOCKS = N // BLOCK
-BLOCKS_IN_PIECE = PIECE // BLOCK
+PIECES = ((0, BLOCK), (BLOCK, BLOCK), (2 * BLOCK, 2 * BLOCK))
+BANK = 512
+VECTOR_SUMSQ_BLOCKS = 2
+VECTOR_MOVED_BLOCKS = 1
 FLOPS = 2 * P * P * N
 
 
@@ -28,7 +29,7 @@ def tile_egnn_kernel(tc, base, f1, nb, nodes, w_gate, b_gate, hs, hb, wv, offs, 
         tc.tile_pool(name="held", bufs=1) as held,
         tc.tile_pool(name="work", bufs=BLOCKS) as work,
         tc.psum_pool(name="psum", bufs=2) as psum,
-        tc.psum_pool(name="psum_moved", bufs=BLOCKS_IN_PIECE * T) as psum_moved,
+        tc.psum_pool(name="psum_moved", bufs=2 * T) as psum_moved,
     ):
         offsets = held.tile([P, N // 16], U16, name="offsets")
         nc.sync.dma_start(offsets[:], offs)
@@ -61,14 +62,14 @@ def tile_egnn_kernel(tc, base, f1, nb, nodes, w_gate, b_gate, hs, hb, wv, offs, 
             nc.sync.dma_start(window[:], base[t * P : (t + 1) * P, :])
             windows.append(window)
 
-        gates = []
-        for piece in range(PIECES):
-            cols = slice(piece * PIECE, (piece + 1) * PIECE)
-            logits = psum.tile([P, PIECE], F32, name="logits", tag="bank")
-            nc.tensor.matmul(logits[:], w_sb[:], nodes_sb[:, cols], start=True, stop=True)
-            gate = held.tile([P, PIECE], F32, name=f"gate{piece}")
-            nc.scalar.activation(gate[:], logits[:], ACT.Sigmoid, bias=b_sb[:])
-            gates.append(gate)
+        gate = held.tile([P, N], F32, name="gate")
+        for first in range(0, N, BANK):
+            logits = psum.tile([P, BANK], F32, name="logits", tag="bank")
+            nc.tensor.matmul(logits[:], w_sb[:], nodes_sb[:, first : first + BANK], start=True, stop=True)
+            nc.scalar.activation(gate[:, first : first + BANK], logits[:], ACT.Sigmoid, bias=b_sb[:])
+
+        table_warmer = held.tile([P, 1], F32, name="table_warmer")
+        nc.scalar.activation(table_warmer[:], gate[:, N - 1 : N], ACT.Abs_reciprocal_sqrt)
 
         slope = held.tile([P, 1], F32, name="slope")
         nc.vector.tensor_tensor(slope[:], hb_sb[:], wv_sb[:], ALU.mult)
@@ -78,15 +79,15 @@ def tile_egnn_kernel(tc, base, f1, nb, nodes, w_gate, b_gate, hs, hb, wv, offs, 
         ident = held.tile([P, P], F32, name="ident")
         make_identity(nc, ident[:])
 
-        moved = [held.tile([P, T, PIECE], F32, name=f"moved{piece}") for piece in range(PIECES)]
+
+        rel_sb = []
+        sumsq_of = []
         for block in range(BLOCKS):
-            piece, first = divmod(block * BLOCK, PIECE)
-            f1_block = f1_sb[block]
             rel = work.tile([P, T, BLOCK], F32, name="rel")
-            nc.vector.tensor_tensor(rel[:], f1_block[:], nb_sb[block][:], ALU.subtract)
+            nc.vector.tensor_tensor(rel[:], f1_sb[block][:], nb_sb[block][:], ALU.subtract)
             squares = work.tile([P, T, BLOCK], F32, name="squares")
             nc.scalar.activation(squares[:], rel[:], ACT.Square)
-            if piece == 0:
+            if block < VECTOR_SUMSQ_BLOCKS:
                 pair = work.tile([P, BLOCK], F32, name="pair")
                 nc.vector.tensor_tensor(pair[:], squares[:, 0, :], squares[:, 1, :], ALU.add)
                 sumsq = work.tile([P, BLOCK], F32, name="sumsq_sb")
@@ -95,28 +96,44 @@ def tile_egnn_kernel(tc, base, f1, nb, nodes, w_gate, b_gate, hs, hb, wv, offs, 
                 sumsq = psum.tile([P, BLOCK], F32, name="sumsq_ps", tag="bank")
                 for t in range(T):
                     nc.tensor.matmul(sumsq[:], ident[:], squares[:, t, :], start=(t == 0), stop=(t == T - 1))
+            rel_sb.append(rel)
+            sumsq_of.append(sumsq)
+
+        upd_sb = []
+        for block in range(BLOCKS):
             inv_nrm = work.tile([P, BLOCK], F32, name="inv_nrm")
-            nc.scalar.activation(inv_nrm[:], sumsq[:], ACT.Abs_reciprocal_sqrt)
+            nc.scalar.activation(inv_nrm[:], sumsq_of[block][:], ACT.Abs_reciprocal_sqrt)
             factor = work.tile([P, BLOCK], F32, name="factor")
             nc.scalar.activation(factor[:], inv_nrm[:], ACT.Identity, bias=level[:], scale=slope[:])
             upd = work.tile([P, T, BLOCK], F32, name="upd")
             nc.vector.tensor_tensor(
-                upd[:], rel[:], factor[:].unsqueeze(1).to_broadcast([P, T, BLOCK]), ALU.mult
+                upd[:], rel_sb[block][:], factor[:].unsqueeze(1).to_broadcast([P, T, BLOCK]), ALU.mult
             )
-            if piece == 0:
-                nc.vector.tensor_tensor(moved[piece][:, :, first : first + BLOCK], f1_block[:], upd[:], ALU.add)
+            upd_sb.append(upd)
+
+        moved_sb = [held.tile([P, T, entries], F32, name=f"moved{first}") for first, entries in PIECES]
+        for block in range(BLOCKS):
+            piece = min(block, len(PIECES) - 1)
+            at = block * BLOCK - PIECES[piece][0]
+            if block < VECTOR_MOVED_BLOCKS:
+                nc.vector.tensor_tensor(
+                    moved_sb[piece][:, :, at : at + BLOCK], f1_sb[block][:], upd_sb[block][:], ALU.add
+                )
             else:
                 for t in range(T):
                     moved_ps = psum_moved.tile([P, BLOCK], F32, name="moved_ps")
-                    nc.tensor.matmul(moved_ps[:], ident[:], f1_block[:, t, :], start=True, stop=False)
-                    nc.tensor.matmul(moved_ps[:], ident[:], upd[:, t, :], start=False, stop=True)
-                    nc.scalar.copy(moved[piece][:, t, first : first + BLOCK], moved_ps[:])
+                    nc.tensor.matmul(moved_ps[:], ident[:], f1_sb[block][:, t, :], start=True, stop=False)
+                    nc.tensor.matmul(moved_ps[:], ident[:], upd_sb[block][:, t, :], start=False, stop=True)
+                    nc.scalar.copy(moved_sb[piece][:, t, at : at + BLOCK], moved_ps[:])
 
-        for piece in range(PIECES):
-            piece_offsets = offsets[:, piece * (PIECE // 16) : (piece + 1) * (PIECE // 16)]
+        for piece, (first, entries) in enumerate(PIECES):
+            piece_offsets = offsets[:, first // 16 : (first + entries) // 16]
             for t in range(T):
                 nc.vector.tensor_tensor(
-                    windows[t][:].indirect(piece_offsets), moved[piece][:, t, :], gates[piece][:], ALU.mult
+                    windows[t][:].indirect(piece_offsets),
+                    moved_sb[piece][:, t, :],
+                    gate[:, first : first + entries],
+                    ALU.mult,
                 )
-                if piece == PIECES - 1:
+                if piece == len(PIECES) - 1:
                     nc.sync.dma_start(out[t * P : (t + 1) * P, :], windows[t][:])

@@ -13,10 +13,13 @@ S = 2048
 N = 1024
 BLOCK = 256
 BLOCKS = N // BLOCK
-PIECES = ((0, BLOCK), (BLOCK, BLOCK), (2 * BLOCK, 2 * BLOCK))
+HALF = N // 2
+PIECES_EARLY_WINDOW = ((0, BLOCK), (BLOCK, BLOCK), (HALF, HALF))
+PIECES_LAST_WINDOW = ((0, HALF), (HALF, HALF))
 BANK = 512
-VECTOR_SUMSQ_BLOCKS = 2
+VECTOR_SUMSQ_BLOCKS = 1
 VECTOR_MOVED_BLOCKS = 1
+VECTOR_FACTOR_BLOCKS = 2
 FLOPS = 2 * P * P * N
 
 
@@ -104,36 +107,37 @@ def tile_egnn_kernel(tc, base, f1, nb, nodes, w_gate, b_gate, hs, hb, wv, offs, 
             inv_nrm = work.tile([P, BLOCK], F32, name="inv_nrm")
             nc.scalar.activation(inv_nrm[:], sumsq_of[block][:], ACT.Abs_reciprocal_sqrt)
             factor = work.tile([P, BLOCK], F32, name="factor")
-            nc.scalar.activation(factor[:], inv_nrm[:], ACT.Identity, bias=level[:], scale=slope[:])
+            if block < VECTOR_FACTOR_BLOCKS:
+                nc.vector.tensor_scalar(factor[:], inv_nrm[:], slope[:], level[:], ALU.mult, ALU.add)
+            else:
+                nc.scalar.activation(factor[:], inv_nrm[:], ACT.Identity, bias=level[:], scale=slope[:])
             upd = work.tile([P, T, BLOCK], F32, name="upd")
             nc.vector.tensor_tensor(
                 upd[:], rel_sb[block][:], factor[:].unsqueeze(1).to_broadcast([P, T, BLOCK]), ALU.mult
             )
             upd_sb.append(upd)
 
-        moved_sb = [held.tile([P, T, entries], F32, name=f"moved{first}") for first, entries in PIECES]
+        moved_sb = [held.tile([P, T, HALF], F32, name=f"moved{half}") for half in range(N // HALF)]
         for block in range(BLOCKS):
-            piece = min(block, len(PIECES) - 1)
-            at = block * BLOCK - PIECES[piece][0]
+            half, at = divmod(block * BLOCK, HALF)
             if block < VECTOR_MOVED_BLOCKS:
                 nc.vector.tensor_tensor(
-                    moved_sb[piece][:, :, at : at + BLOCK], f1_sb[block][:], upd_sb[block][:], ALU.add
+                    moved_sb[half][:, :, at : at + BLOCK], f1_sb[block][:], upd_sb[block][:], ALU.add
                 )
             else:
                 for t in range(T):
                     moved_ps = psum_moved.tile([P, BLOCK], F32, name="moved_ps")
                     nc.tensor.matmul(moved_ps[:], ident[:], f1_sb[block][:, t, :], start=True, stop=False)
                     nc.tensor.matmul(moved_ps[:], ident[:], upd_sb[block][:, t, :], start=False, stop=True)
-                    nc.scalar.copy(moved_sb[piece][:, t, at : at + BLOCK], moved_ps[:])
+                    nc.scalar.copy(moved_sb[half][:, t, at : at + BLOCK], moved_ps[:])
 
-        for piece, (first, entries) in enumerate(PIECES):
-            piece_offsets = offsets[:, first // 16 : (first + entries) // 16]
-            for t in range(T):
+        for t in range(T):
+            for first, entries in PIECES_LAST_WINDOW if t == T - 1 else PIECES_EARLY_WINDOW:
+                half, at = divmod(first, HALF)
                 nc.vector.tensor_tensor(
-                    windows[t][:].indirect(piece_offsets),
-                    moved_sb[piece][:, t, :],
+                    windows[t][:].indirect(offsets[:, first // 16 : (first + entries) // 16]),
+                    moved_sb[half][:, t, at : at + entries],
                     gate[:, first : first + entries],
                     ALU.mult,
                 )
-                if piece == len(PIECES) - 1:
-                    nc.sync.dma_start(out[t * P : (t + 1) * P, :], windows[t][:])
+            nc.sync.dma_start(out[t * P : (t + 1) * P, :], windows[t][:])

@@ -82,14 +82,19 @@ def tile_egnn_kernel(tc, base, f1, nb, nodes, w_gate, b_gate, hs, hb, wv, offs, 
         ident = held.tile([P, P], F32, name="ident")
         make_identity(nc, ident[:])
 
-
         rel_sb = []
         sumsq_of = []
-        for block in range(BLOCKS):
+        upd_sb = []
+        moved_sb = [held.tile([P, T, HALF], F32, name=f"moved{half}") for half in range(N // HALF)]
+
+        def stage_sum_of_squares(block):
             rel = work.tile([P, T, BLOCK], F32, name="rel")
             nc.vector.tensor_tensor(rel[:], f1_sb[block][:], nb_sb[block][:], ALU.subtract)
             squares = work.tile([P, T, BLOCK], F32, name="squares")
-            nc.scalar.activation(squares[:], rel[:], ACT.Square)
+            if block == 1:
+                nc.vector.tensor_tensor(squares[:], rel[:], rel[:], ALU.mult)
+            else:
+                nc.scalar.activation(squares[:], rel[:], ACT.Square)
             if block < VECTOR_SUMSQ_BLOCKS:
                 pair = work.tile([P, BLOCK], F32, name="pair")
                 nc.vector.tensor_tensor(pair[:], squares[:, 0, :], squares[:, 1, :], ALU.add)
@@ -102,8 +107,7 @@ def tile_egnn_kernel(tc, base, f1, nb, nodes, w_gate, b_gate, hs, hb, wv, offs, 
             rel_sb.append(rel)
             sumsq_of.append(sumsq)
 
-        upd_sb = []
-        for block in range(BLOCKS):
+        def stage_product(block):
             inv_nrm = work.tile([P, BLOCK], F32, name="inv_nrm")
             nc.scalar.activation(inv_nrm[:], sumsq_of[block][:], ACT.Abs_reciprocal_sqrt)
             factor = work.tile([P, BLOCK], F32, name="factor")
@@ -117,8 +121,7 @@ def tile_egnn_kernel(tc, base, f1, nb, nodes, w_gate, b_gate, hs, hb, wv, offs, 
             )
             upd_sb.append(upd)
 
-        moved_sb = [held.tile([P, T, HALF], F32, name=f"moved{half}") for half in range(N // HALF)]
-        for block in range(BLOCKS):
+        def stage_moved(block):
             half, at = divmod(block * BLOCK, HALF)
             if block < VECTOR_MOVED_BLOCKS:
                 nc.vector.tensor_tensor(
@@ -130,6 +133,14 @@ def tile_egnn_kernel(tc, base, f1, nb, nodes, w_gate, b_gate, hs, hb, wv, offs, 
                     nc.tensor.matmul(moved_ps[:], ident[:], f1_sb[block][:, t, :], start=True, stop=False)
                     nc.tensor.matmul(moved_ps[:], ident[:], upd_sb[block][:, t, :], start=False, stop=True)
                     nc.scalar.copy(moved_sb[half][:, t, at : at + BLOCK], moved_ps[:])
+
+        for step in range(BLOCKS + 2):
+            if step < BLOCKS:
+                stage_sum_of_squares(step)
+            if 0 <= step - 1 < BLOCKS:
+                stage_product(step - 1)
+            if 0 <= step - 2 < BLOCKS:
+                stage_moved(step - 2)
 
         for t in range(T):
             for first, entries in PIECES_LAST_WINDOW if t == T - 1 else PIECES_EARLY_WINDOW:

@@ -11,12 +11,12 @@ P = 128
 T = 3
 S = 2048
 N = 1024
-BLOCK = 256
-BLOCKS = N // BLOCK
 HALF = N // 2
-PIECES_EARLY_WINDOW = ((0, BLOCK), (BLOCK, BLOCK), (HALF, HALF))
+BLOCK = 256
+BLOCKS = tuple((at, BLOCK) for at in range(0, N, BLOCK))
+PIECES_EARLY_WINDOW = ((0, HALF // 2), (HALF // 2, HALF // 2), (HALF, HALF))
 PIECES_LAST_WINDOW = ((0, HALF), (HALF, HALF))
-BANK = 512
+VECTOR_SQUARES_BLOCKS = 1
 VECTOR_SUMSQ_BLOCKS = 1
 VECTOR_MOVED_BLOCKS = 1
 VECTOR_FACTOR_BLOCKS = 2
@@ -30,54 +30,76 @@ def tile_egnn_kernel(tc, base, f1, nb, nodes, w_gate, b_gate, hs, hb, wv, offs, 
 
     with (
         tc.tile_pool(name="held", bufs=1) as held,
-        tc.tile_pool(name="work", bufs=BLOCKS) as work,
-        tc.psum_pool(name="psum", bufs=2) as psum,
-        tc.psum_pool(name="psum_moved", bufs=2 * T) as psum_moved,
+        tc.tile_pool(name="work", bufs=len(BLOCKS)) as work,
+        tc.psum_pool(name="psum_gate", bufs=1) as psum_gate,
+        tc.psum_pool(name="psum_sumsq", bufs=2) as psum_sumsq,
+        tc.psum_pool(name="psum_moved", bufs=5) as psum_moved,
     ):
-        offsets = held.tile([P, N // 16], U16, name="offsets")
-        nc.sync.dma_start(offsets[:], offs)
+        zero = held.tile([P, 1], F32, name="zero")
+        nc.vector.memset(zero[:], 0.0)
+        sigmoid_warmer = held.tile([P, 1], F32, name="sigmoid_warmer")
+        nc.scalar.activation(sigmoid_warmer[:], zero[:], ACT.Sigmoid)
 
         w_sb = held.tile([P, P], BF16, name="w_sb")
         nc.sync.dma_start(w_sb[:], w_gate)
-        nodes_sb = held.tile([P, N], BF16, name="nodes_sb")
-        nc.sync.dma_start(nodes_sb[:], nodes)
         b_sb = held.tile([P, 1], F32, name="b_sb")
-        nc.scalar.dma_start(b_sb[:], b_gate)
+        nc.sync.dma_start(b_sb[:], b_gate)
         hs_sb = held.tile([P, 1], F32, name="hs_sb")
         nc.scalar.dma_start(hs_sb[:], hs)
         hb_sb = held.tile([P, 1], F32, name="hb_sb")
         nc.scalar.dma_start(hb_sb[:], hb)
         wv_sb = held.tile([P, 1], F32, name="wv_sb")
         nc.scalar.dma_start(wv_sb[:], wv)
+
+        nodes_sb = held.tile([P, N], BF16, name="nodes_sb")
         f1_sb = []
         nb_sb = []
-        for block in range(BLOCKS):
-            cols = slice(block * BLOCK, (block + 1) * BLOCK)
-            f1_block = work.tile([P, T, BLOCK], F32, name="f1_block")
-            nc.sync.dma_start(f1_block[:], f1_dtn[:, :, cols])
-            nb_block = work.tile([P, T, BLOCK], F32, name="nb_block")
-            nc.sync.dma_start(nb_block[:], nb_dtn[:, :, cols])
+        windows = []
+
+        def load_nodes(first):
+            nc.sync.dma_start(nodes_sb[:, first : first + HALF], nodes[:, first : first + HALF])
+
+        def load_features(first, columns):
+            f1_block = work.tile([P, T, columns], F32, name="f1_block")
+            nc.sync.dma_start(f1_block[:], f1_dtn[:, :, first : first + columns])
+            nb_block = work.tile([P, T, columns], F32, name="nb_block")
+            nc.sync.dma_start(nb_block[:], nb_dtn[:, :, first : first + columns])
             f1_sb.append(f1_block)
             nb_sb.append(nb_block)
-        windows = []
-        for t in range(T):
+
+        def load_window(t):
             window = held.tile([P, S], F32, name=f"window{t}")
             nc.sync.dma_start(window[:], base[t * P : (t + 1) * P, :])
             windows.append(window)
 
-        gate = held.tile([P, N], F32, name="gate")
-        for first in range(0, N, BANK):
-            logits = psum.tile([P, BANK], F32, name="logits", tag="bank")
-            nc.tensor.matmul(logits[:], w_sb[:], nodes_sb[:, first : first + BANK], start=True, stop=True)
-            nc.scalar.activation(gate[:, first : first + BANK], logits[:], ACT.Sigmoid, bias=b_sb[:])
+        load_nodes(0)
+        for first, columns in BLOCKS:
+            load_features(first, columns)
+        offsets = held.tile([P, N // 16], U16, name="offsets")
+        nc.sync.dma_start(offsets[:], offs)
+        load_window(0)
+        load_window(1)
+        load_nodes(HALF)
+        load_window(2)
+
+        gate_sb = []
+
+        def make_gate(first):
+            logits = psum_gate.tile([P, HALF], F32, name="logits")
+            nc.tensor.matmul(logits[:], w_sb[:], nodes_sb[:, first : first + HALF], start=True, stop=True)
+            gate = held.tile([P, HALF], F32, name=f"gate{first}")
+            nc.scalar.activation(gate[:], logits[:], ACT.Sigmoid, bias=b_sb[:])
+            gate_sb.append(gate)
+
+        make_gate(0)
 
         table_warmer = held.tile([P, 1], F32, name="table_warmer")
-        nc.scalar.activation(table_warmer[:], gate[:, N - 1 : N], ACT.Abs_reciprocal_sqrt)
+        nc.scalar.activation(table_warmer[:], gate_sb[0][:, HALF - 1 : HALF], ACT.Abs_reciprocal_sqrt)
 
         slope = held.tile([P, 1], F32, name="slope")
-        nc.vector.tensor_tensor(slope[:], hb_sb[:], wv_sb[:], ALU.mult)
+        nc.gpsimd.tensor_tensor(slope[:], hb_sb[:], wv_sb[:], ALU.mult)
         level = held.tile([P, 1], F32, name="level")
-        nc.vector.tensor_tensor(level[:], hs_sb[:], wv_sb[:], ALU.mult)
+        nc.gpsimd.tensor_tensor(level[:], hs_sb[:], wv_sb[:], ALU.mult)
 
         ident = held.tile([P, P], F32, name="ident")
         make_identity(nc, ident[:])
@@ -88,58 +110,64 @@ def tile_egnn_kernel(tc, base, f1, nb, nodes, w_gate, b_gate, hs, hb, wv, offs, 
         moved_sb = [held.tile([P, T, HALF], F32, name=f"moved{half}") for half in range(N // HALF)]
 
         def stage_sum_of_squares(block):
-            rel = work.tile([P, T, BLOCK], F32, name="rel")
+            columns = BLOCKS[block][1]
+            rel = work.tile([P, T, columns], F32, name="rel")
             nc.vector.tensor_tensor(rel[:], f1_sb[block][:], nb_sb[block][:], ALU.subtract)
-            squares = work.tile([P, T, BLOCK], F32, name="squares")
-            if block == 1:
+            squares = work.tile([P, T, columns], F32, name="squares")
+            if block < VECTOR_SQUARES_BLOCKS:
                 nc.vector.tensor_tensor(squares[:], rel[:], rel[:], ALU.mult)
             else:
                 nc.scalar.activation(squares[:], rel[:], ACT.Square)
             if block < VECTOR_SUMSQ_BLOCKS:
-                pair = work.tile([P, BLOCK], F32, name="pair")
+                pair = work.tile([P, columns], F32, name="pair")
                 nc.vector.tensor_tensor(pair[:], squares[:, 0, :], squares[:, 1, :], ALU.add)
-                sumsq = work.tile([P, BLOCK], F32, name="sumsq_sb")
+                sumsq = work.tile([P, columns], F32, name="sumsq_sb")
                 nc.vector.tensor_tensor(sumsq[:], pair[:], squares[:, 2, :], ALU.add)
             else:
-                sumsq = psum.tile([P, BLOCK], F32, name="sumsq_ps", tag="bank")
+                sumsq = psum_sumsq.tile([P, columns], F32, name="sumsq_ps")
                 for t in range(T):
                     nc.tensor.matmul(sumsq[:], ident[:], squares[:, t, :], start=(t == 0), stop=(t == T - 1))
             rel_sb.append(rel)
             sumsq_of.append(sumsq)
 
         def stage_product(block):
-            inv_nrm = work.tile([P, BLOCK], F32, name="inv_nrm")
+            columns = BLOCKS[block][1]
+            inv_nrm = work.tile([P, columns], F32, name="inv_nrm")
             nc.scalar.activation(inv_nrm[:], sumsq_of[block][:], ACT.Abs_reciprocal_sqrt)
-            factor = work.tile([P, BLOCK], F32, name="factor")
+            factor = work.tile([P, columns], F32, name="factor")
             if block < VECTOR_FACTOR_BLOCKS:
                 nc.vector.tensor_scalar(factor[:], inv_nrm[:], slope[:], level[:], ALU.mult, ALU.add)
             else:
                 nc.scalar.activation(factor[:], inv_nrm[:], ACT.Identity, bias=level[:], scale=slope[:])
-            upd = work.tile([P, T, BLOCK], F32, name="upd")
+            upd = work.tile([P, T, columns], F32, name="upd")
             nc.vector.tensor_tensor(
-                upd[:], rel_sb[block][:], factor[:].unsqueeze(1).to_broadcast([P, T, BLOCK]), ALU.mult
+                upd[:], rel_sb[block][:], factor[:].unsqueeze(1).to_broadcast([P, T, columns]), ALU.mult
             )
             upd_sb.append(upd)
 
         def stage_moved(block):
-            half, at = divmod(block * BLOCK, HALF)
+            first, columns = BLOCKS[block]
+            half, at = divmod(first, HALF)
             if block < VECTOR_MOVED_BLOCKS:
                 nc.vector.tensor_tensor(
-                    moved_sb[half][:, :, at : at + BLOCK], f1_sb[block][:], upd_sb[block][:], ALU.add
+                    moved_sb[half][:, :, at : at + columns], f1_sb[block][:], upd_sb[block][:], ALU.add
                 )
             else:
                 for t in range(T):
-                    moved_ps = psum_moved.tile([P, BLOCK], F32, name="moved_ps")
+                    moved_ps = psum_moved.tile([P, columns], F32, name="moved_ps")
                     nc.tensor.matmul(moved_ps[:], ident[:], f1_sb[block][:, t, :], start=True, stop=False)
                     nc.tensor.matmul(moved_ps[:], ident[:], upd_sb[block][:, t, :], start=False, stop=True)
-                    nc.scalar.copy(moved_sb[half][:, t, at : at + BLOCK], moved_ps[:])
+                    nc.scalar.copy(moved_sb[half][:, t, at : at + columns], moved_ps[:])
 
-        for step in range(BLOCKS + 2):
-            if step < BLOCKS:
+        last = len(BLOCKS) - 1
+        for step in range(len(BLOCKS) + 2):
+            if step <= last:
                 stage_sum_of_squares(step)
-            if 0 <= step - 1 < BLOCKS:
+            if 0 <= step - 1 <= last:
                 stage_product(step - 1)
-            if 0 <= step - 2 < BLOCKS:
+            if step - 1 == last:
+                make_gate(HALF)
+            if 0 <= step - 2 <= last:
                 stage_moved(step - 2)
 
         for t in range(T):
@@ -148,7 +176,7 @@ def tile_egnn_kernel(tc, base, f1, nb, nodes, w_gate, b_gate, hs, hb, wv, offs, 
                 nc.vector.tensor_tensor(
                     windows[t][:].indirect(offsets[:, first // 16 : (first + entries) // 16]),
                     moved_sb[half][:, t, at : at + entries],
-                    gate[:, first : first + entries],
+                    gate_sb[half][:, at : at + entries],
                     ALU.mult,
                 )
             nc.sync.dma_start(out[t * P : (t + 1) * P, :], windows[t][:])

@@ -19,7 +19,7 @@ PIECES_LAST_WINDOW = ((0, HALF), (HALF, HALF))
 VECTOR_SQUARES_BLOCKS = 1
 VECTOR_SUMSQ_BLOCKS = 1
 VECTOR_MOVED_BLOCKS = 1
-VECTOR_FACTOR_BLOCKS = 2
+VECTOR_FACTOR_BLOCKS = 1
 FLOPS = 2 * P * P * N
 
 

import concourse.mybir as mybir
from concourse.masks import make_identity

F32 = mybir.dt.float32
BF16 = mybir.dt.bfloat16
U16 = mybir.dt.uint16
ALU = mybir.AluOpType
ACT = mybir.ActivationFunctionType

P = 128
T = 3
S = 2048
N = 1024
HALF = N // 2
BLOCK = 256
BLOCKS = tuple((at, BLOCK) for at in range(0, N, BLOCK))
PIECES_EARLY_WINDOW = ((0, HALF // 2), (HALF // 2, HALF // 2), (HALF, HALF))
PIECES_LAST_WINDOW = ((0, HALF), (HALF, HALF))
VECTOR_SQUARES_BLOCKS = 1
VECTOR_SUMSQ_BLOCKS = 1
VECTOR_MOVED_BLOCKS = 1
VECTOR_FACTOR_BLOCKS = 1
FLOPS = 2 * P * P * N


def tile_egnn_kernel(tc, base, f1, nb, nodes, w_gate, b_gate, hs, hb, wv, offs, out):
    nc = tc.nc
    f1_dtn = f1.rearrange("(t d) n -> d t n", t=T)
    nb_dtn = nb.rearrange("(t d) n -> d t n", t=T)

    with (
        tc.tile_pool(name="held", bufs=1) as held,
        tc.tile_pool(name="work", bufs=len(BLOCKS)) as work,
        tc.psum_pool(name="psum_gate", bufs=1) as psum_gate,
        tc.psum_pool(name="psum_sumsq", bufs=2) as psum_sumsq,
        tc.psum_pool(name="psum_moved", bufs=5) as psum_moved,
    ):
        zero = held.tile([P, 1], F32, name="zero")
        nc.vector.memset(zero[:], 0.0)
        sigmoid_warmer = held.tile([P, 1], F32, name="sigmoid_warmer")
        nc.scalar.activation(sigmoid_warmer[:], zero[:], ACT.Sigmoid)

        w_sb = held.tile([P, P], BF16, name="w_sb")
        nc.sync.dma_start(w_sb[:], w_gate)
        b_sb = held.tile([P, 1], F32, name="b_sb")
        nc.sync.dma_start(b_sb[:], b_gate)
        hs_sb = held.tile([P, 1], F32, name="hs_sb")
        nc.scalar.dma_start(hs_sb[:], hs)
        hb_sb = held.tile([P, 1], F32, name="hb_sb")
        nc.scalar.dma_start(hb_sb[:], hb)
        wv_sb = held.tile([P, 1], F32, name="wv_sb")
        nc.scalar.dma_start(wv_sb[:], wv)

        nodes_sb = held.tile([P, N], BF16, name="nodes_sb")
        f1_sb = []
        nb_sb = []
        windows = []

        def load_nodes(first):
            nc.sync.dma_start(nodes_sb[:, first : first + HALF], nodes[:, first : first + HALF])

        def load_features(first, columns):
            f1_block = work.tile([P, T, columns], F32, name="f1_block")
            nc.sync.dma_start(f1_block[:], f1_dtn[:, :, first : first + columns])
            nb_block = work.tile([P, T, columns], F32, name="nb_block")
            nc.sync.dma_start(nb_block[:], nb_dtn[:, :, first : first + columns])
            f1_sb.append(f1_block)
            nb_sb.append(nb_block)

        def load_window(t):
            window = held.tile([P, S], F32, name=f"window{t}")
            nc.sync.dma_start(window[:], base[t * P : (t + 1) * P, :])
            windows.append(window)

        load_nodes(0)
        for first, columns in BLOCKS:
            load_features(first, columns)
        offsets = held.tile([P, N // 16], U16, name="offsets")
        nc.sync.dma_start(offsets[:], offs)
        load_window(0)
        load_window(1)
        load_nodes(HALF)
        load_window(2)

        gate_sb = []

        def make_gate(first):
            logits = psum_gate.tile([P, HALF], F32, name="logits")
            nc.tensor.matmul(logits[:], w_sb[:], nodes_sb[:, first : first + HALF], start=True, stop=True)
            gate = held.tile([P, HALF], F32, name=f"gate{first}")
            nc.scalar.activation(gate[:], logits[:], ACT.Sigmoid, bias=b_sb[:])
            gate_sb.append(gate)

        make_gate(0)

        table_warmer = held.tile([P, 1], F32, name="table_warmer")
        nc.scalar.activation(table_warmer[:], gate_sb[0][:, HALF - 1 : HALF], ACT.Abs_reciprocal_sqrt)

        slope = held.tile([P, 1], F32, name="slope")
        nc.gpsimd.tensor_tensor(slope[:], hb_sb[:], wv_sb[:], ALU.mult)
        level = held.tile([P, 1], F32, name="level")
        nc.gpsimd.tensor_tensor(level[:], hs_sb[:], wv_sb[:], ALU.mult)

        ident = held.tile([P, P], F32, name="ident")
        make_identity(nc, ident[:])

        rel_sb = []
        sumsq_of = []
        upd_sb = []
        moved_sb = [held.tile([P, T, HALF], F32, name=f"moved{half}") for half in range(N // HALF)]

        def stage_sum_of_squares(block):
            columns = BLOCKS[block][1]
            rel = work.tile([P, T, columns], F32, name="rel")
            nc.vector.tensor_tensor(rel[:], f1_sb[block][:], nb_sb[block][:], ALU.subtract)
            squares = work.tile([P, T, columns], F32, name="squares")
            if block < VECTOR_SQUARES_BLOCKS:
                nc.vector.tensor_tensor(squares[:], rel[:], rel[:], ALU.mult)
            else:
                nc.scalar.activation(squares[:], rel[:], ACT.Square)
            if block < VECTOR_SUMSQ_BLOCKS:
                pair = work.tile([P, columns], F32, name="pair")
                nc.vector.tensor_tensor(pair[:], squares[:, 0, :], squares[:, 1, :], ALU.add)
                sumsq = work.tile([P, columns], F32, name="sumsq_sb")
                nc.vector.tensor_tensor(sumsq[:], pair[:], squares[:, 2, :], ALU.add)
            else:
                sumsq = psum_sumsq.tile([P, columns], F32, name="sumsq_ps")
                for t in range(T):
                    nc.tensor.matmul(sumsq[:], ident[:], squares[:, t, :], start=(t == 0), stop=(t == T - 1))
            rel_sb.append(rel)
            sumsq_of.append(sumsq)

        def stage_product(block):
            columns = BLOCKS[block][1]
            inv_nrm = work.tile([P, columns], F32, name="inv_nrm")
            nc.scalar.activation(inv_nrm[:], sumsq_of[block][:], ACT.Abs_reciprocal_sqrt)
            factor = work.tile([P, columns], F32, name="factor")
            if block < VECTOR_FACTOR_BLOCKS:
                nc.vector.tensor_scalar(factor[:], inv_nrm[:], slope[:], level[:], ALU.mult, ALU.add)
            else:
                nc.scalar.activation(factor[:], inv_nrm[:], ACT.Identity, bias=level[:], scale=slope[:])
            upd = work.tile([P, T, columns], F32, name="upd")
            nc.vector.tensor_tensor(
                upd[:], rel_sb[block][:], factor[:].unsqueeze(1).to_broadcast([P, T, columns]), ALU.mult
            )
            upd_sb.append(upd)

        def stage_moved(block):
            first, columns = BLOCKS[block]
            half, at = divmod(first, HALF)
            if block < VECTOR_MOVED_BLOCKS:
                nc.vector.tensor_tensor(
                    moved_sb[half][:, :, at : at + columns], f1_sb[block][:], upd_sb[block][:], ALU.add
                )
            else:
                for t in range(T):
                    moved_ps = psum_moved.tile([P, columns], F32, name="moved_ps")
                    nc.tensor.matmul(moved_ps[:], ident[:], f1_sb[block][:, t, :], start=True, stop=False)
                    nc.tensor.matmul(moved_ps[:], ident[:], upd_sb[block][:, t, :], start=False, stop=True)
                    nc.scalar.copy(moved_sb[half][:, t, at : at + columns], moved_ps[:])

        last = len(BLOCKS) - 1
        for step in range(len(BLOCKS) + 2):
            if step <= last:
                stage_sum_of_squares(step)
            if 0 <= step - 1 <= last:
                stage_product(step - 1)
            if step - 1 == last:
                make_gate(HALF)
            if 0 <= step - 2 <= last:
                stage_moved(step - 2)

        for t in range(T):
            for first, entries in PIECES_LAST_WINDOW if t == T - 1 else PIECES_EARLY_WINDOW:
                half, at = divmod(first, HALF)
                nc.vector.tensor_tensor(
                    windows[t][:].indirect(offsets[:, first // 16 : (first + entries) // 16]),
                    moved_sb[half][:, t, at : at + entries],
                    gate_sb[half][:, at : at + entries],
                    ALU.mult,
                )
            nc.sync.dma_start(out[t * P : (t + 1) * P, :], windows[t][:])
